import numpy as np
import ml_dtypes

BF16 = ml_dtypes.bfloat16


def bf(x):
    return np.asarray(x, np.float32).astype(BF16)


def f32(x):
    return np.asarray(x, np.float32)


def f64(x):
    return np.asarray(x).astype(np.float64)


def striped(idx):
    return np.tile(idx.reshape(-1, 16).T, (8, 1))


C, S, N = 768, 1024, 128
W_SCALE = 0.02


def erf(a):
    t = np.clip(a, -6.0, 6.0)
    term = t.copy()
    total = t.copy()
    for n in range(1, 150):
        term = term * 2.0 * t * t / (2 * n + 1)
        total = total + term
    r = 2.0 / np.sqrt(np.pi) * np.exp(-t * t) * total
    return np.where(np.abs(a) > 6.0, np.sign(a), r)


def gelu_erf(v):
    return 0.5 * v * (1.0 + erf(v / np.sqrt(2.0)))


def setup_inputs():
    return {"hidden": bf(np.random.standard_normal((C, N))), "table": f32(np.random.standard_normal((C, S))), "wd": bf(W_SCALE * np.random.standard_normal((C, C))), "bd": f32(0.1 * np.random.standard_normal((C, 1))), "wc": bf(W_SCALE * np.random.standard_normal((C, C))), "bc": f32(0.1 * np.random.standard_normal((C, 1))), "offs": striped(np.random.permutation(np.tile(np.arange(S), 2))[:N])}


def reference(hidden, table, wd, bd, wc, bc, offs):
    idx = offs[:16].T.reshape(-1)
    picked = f64(table)[:, idx]
    return gelu_erf(f64(wd).T @ f64(hidden) + f64(bd) + f64(wc).T @ picked + f64(bc))

@@ -1,0 +1,66 @@
+import concourse.mybir as mybir
+
+BF16, F32, U16 = mybir.dt.bfloat16, mybir.dt.float32, mybir.dt.uint16
+COPY, GELU = mybir.ActivationFunctionType.Copy, mybir.ActivationFunctionType.Gelu
+
+P = 128
+C = 768
+S = 1024
+N = 128
+BLOCKS = C // P
+
+FLOPS = 2 * 2 * C * C * N
+
+
+def tile_fusionlayer_kernel(tc, hidden, table, wd, bd, wc, bc, offs, out):
+    nc = tc.nc
+    with (
+        tc.tile_pool(name="held", bufs=1) as held,
+        tc.psum_pool(name="sums", bufs=1) as sums,
+    ):
+        offsets = held.tile([P, N // 16], U16, name="offsets")
+        nc.sync.dma_start(offsets[:], offs)
+
+        bias_d = held.tile([P, BLOCKS], F32, name="bias_d")
+        bias_c = held.tile([P, BLOCKS], F32, name="bias_c")
+        with nc.allow_non_contiguous_dma(reason="one bias element to a partition"):
+            nc.sync.dma_start(bias_d[:], bd.rearrange("(b p) o -> p (b o)", p=P))
+            nc.sync.dma_start(bias_c[:], bc.rearrange("(b p) o -> p (b o)", p=P))
+        tokens = held.tile([P, BLOCKS, N], BF16, name="tokens")
+        nc.sync.dma_start(tokens[:], hidden.rearrange("(k p) j -> p k j", p=P))
+
+        dense_w = [held.tile([P, C], BF16, name=f"dense_w{k}") for k in range(BLOCKS)]
+        for k in range(BLOCKS):
+            nc.sync.dma_start(dense_w[k][:], wd[k * P : (k + 1) * P, :])
+
+        window = [held.tile([P, S], F32, name=f"window{k}") for k in range(BLOCKS)]
+        column_w = [held.tile([P, C], BF16, name=f"column_w{k}") for k in range(BLOCKS)]
+        for k in range(BLOCKS):
+            nc.sync.dma_start(window[k][:], table[k * P : (k + 1) * P, :])
+            nc.sync.dma_start(column_w[k][:], wc[k * P : (k + 1) * P, :])
+
+        bias = held.tile([P, BLOCKS], F32, name="bias")
+        nc.vector.tensor_add(bias[:], bias_d[:], bias_c[:])
+
+        total = [sums.tile([P, N], F32, name=f"total{b}") for b in range(BLOCKS)]
+
+        for k in range(BLOCKS):
+            for b in range(BLOCKS):
+                nc.tensor.matmul(
+                    total[b][:], dense_w[k][:, b * P : (b + 1) * P], tokens[:, k, :], start=(k == 0), stop=False
+                )
+
+        for k in range(BLOCKS):
+            picked = held.tile([P, N], F32, name=f"picked{k}")
+            nc.scalar.activation(picked[:], window[k][:].indirect(offsets[:]), COPY)
+            picked_bf = held.tile([P, N], BF16, name=f"picked_bf{k}")
+            nc.vector.tensor_copy(picked_bf[:], picked[:])
+            for b in range(BLOCKS):
+                nc.tensor.matmul(
+                    total[b][:], column_w[k][:, b * P : (b + 1) * P], picked_bf[:], start=False, stop=(k == BLOCKS - 1)
+                )
+
+        for b in range(BLOCKS):
+            result = held.tile([P, N], F32, name=f"result{b}")
+            nc.scalar.activation(result[:], total[b][:], GELU, bias=bias[:, b : b + 1])
+            nc.sync.dma_start(out[b * P : (b + 1) * P, :], result[:])

@@ -8,6 +8,7 @@ C = 768
 S = 1024
 N = 128
 BLOCKS = C // P
+HALF = BLOCKS // 2
 
 FLOPS = 2 * 2 * C * C * N
 
@@ -21,33 +22,41 @@ def tile_fusionlayer_kernel(tc, hidden, table, wd, bd, wc, bc, offs, out):
         offsets = held.tile([P, N // 16], U16, name="offsets")
         nc.sync.dma_start(offsets[:], offs)
 
-        bias_d = held.tile([P, BLOCKS], F32, name="bias_d")
-        bias_c = held.tile([P, BLOCKS], F32, name="bias_c")
-        with nc.allow_non_contiguous_dma(reason="one bias element to a partition"):
-            nc.sync.dma_start(bias_d[:], bd.rearrange("(b p) o -> p (b o)", p=P))
-            nc.sync.dma_start(bias_c[:], bc.rearrange("(b p) o -> p (b o)", p=P))
+        bias_rows = held.tile([2, C], F32, name="bias_rows")
+        nc.sync.dma_start(bias_rows[0:1, :], bd.rearrange("m o -> o m"))
+        nc.sync.dma_start(bias_rows[1:2, :], bc.rearrange("m o -> o m"))
+        ones = held.tile([2, N], F32, name="ones")
+        nc.vector.memset(ones[:], 1.0)
+
         tokens = held.tile([P, BLOCKS, N], BF16, name="tokens")
-        nc.sync.dma_start(tokens[:], hidden.rearrange("(k p) j -> p k j", p=P))
+        nc.sync.dma_start(tokens[:], hidden.rearrange("(p k) j -> p k j", k=BLOCKS))
 
-        dense_w = [held.tile([P, C], BF16, name=f"dense_w{k}") for k in range(BLOCKS)]
-        for k in range(BLOCKS):
-            nc.sync.dma_start(dense_w[k][:], wd[k * P : (k + 1) * P, :])
+        wd_blocks = wd.rearrange("(p k) m -> p k m", k=BLOCKS)
+        dense_w = [held.tile([P, HALF, C], BF16, name=f"dense_w{h}") for h in range(2)]
+        for h in range(2):
+            nc.sync.dma_start(dense_w[h][:], wd_blocks[:, h * HALF : (h + 1) * HALF, :])
 
+        table_blocks = table.rearrange("(p k) s -> p k s", k=BLOCKS)
+        wc_blocks = wc.rearrange("(p k) m -> p k m", k=BLOCKS)
         window = [held.tile([P, S], F32, name=f"window{k}") for k in range(BLOCKS)]
         column_w = [held.tile([P, C], BF16, name=f"column_w{k}") for k in range(BLOCKS)]
         for k in range(BLOCKS):
-            nc.sync.dma_start(window[k][:], table[k * P : (k + 1) * P, :])
-            nc.sync.dma_start(column_w[k][:], wc[k * P : (k + 1) * P, :])
-
-        bias = held.tile([P, BLOCKS], F32, name="bias")
-        nc.vector.tensor_add(bias[:], bias_d[:], bias_c[:])
+            nc.sync.dma_start(window[k][:], table_blocks[:, k, :])
+            nc.sync.dma_start(column_w[k][:], wc_blocks[:, k, :])
 
         total = [sums.tile([P, N], F32, name=f"total{b}") for b in range(BLOCKS)]
+
+        for b in range(BLOCKS):
+            nc.tensor.matmul(total[b][:], bias_rows[:, b * P : (b + 1) * P], ones[:], start=True, stop=False)
 
         for k in range(BLOCKS):
             for b in range(BLOCKS):
                 nc.tensor.matmul(
-                    total[b][:], dense_w[k][:, b * P : (b + 1) * P], tokens[:, k, :], start=(k == 0), stop=False
+                    total[b][:],
+                    dense_w[k // HALF][:, k % HALF, b * P : (b + 1) * P],
+                    tokens[:, k, :],
+                    start=False,
+                    stop=False,
                 )
 
         for k in range(BLOCKS):
@@ -62,5 +71,5 @@ def tile_fusionlayer_kernel(tc, hidden, table, wd, bd, wc, bc, offs, out):
 
         for b in range(BLOCKS):
             result = held.tile([P, N], F32, name=f"result{b}")
-            nc.scalar.activation(result[:], total[b][:], GELU, bias=bias[:, b : b + 1])
+            nc.scalar.activation(result[:], total[b][:], GELU)
             nc.sync.dma_start(out[b * P : (b + 1) * P, :], result[:])

@@ -8,7 +8,6 @@ C = 768
 S = 1024
 N = 128
 BLOCKS = C // P
-HALF = BLOCKS // 2
 
 FLOPS = 2 * 2 * C * C * N
 
@@ -31,18 +30,21 @@ def tile_fusionlayer_kernel(tc, hidden, table, wd, bd, wc, bc, offs, out):
         tokens = held.tile([P, BLOCKS, N], BF16, name="tokens")
         nc.sync.dma_start(tokens[:], hidden.rearrange("(p k) j -> p k j", k=BLOCKS))
 
-        wd_blocks = wd.rearrange("(p k) m -> p k m", k=BLOCKS)
-        dense_w = [held.tile([P, HALF, C], BF16, name=f"dense_w{h}") for h in range(2)]
-        for h in range(2):
-            nc.sync.dma_start(dense_w[h][:], wd_blocks[:, h * HALF : (h + 1) * HALF, :])
-
         table_blocks = table.rearrange("(p k) s -> p k s", k=BLOCKS)
+        wd_blocks = wd.rearrange("(p k) m -> p k m", k=BLOCKS)
         wc_blocks = wc.rearrange("(p k) m -> p k m", k=BLOCKS)
         window = [held.tile([P, S], F32, name=f"window{k}") for k in range(BLOCKS)]
+        dense_w = [held.tile([P, C], BF16, name=f"dense_w{k}") for k in range(BLOCKS)]
         column_w = [held.tile([P, C], BF16, name=f"column_w{k}") for k in range(BLOCKS)]
+
+        nc.sync.dma_start(window[0][:], table_blocks[:, 0, :])
+        nc.sync.dma_start(dense_w[0][:], wd_blocks[:, 0, :])
         for k in range(BLOCKS):
-            nc.sync.dma_start(window[k][:], table_blocks[:, k, :])
+            if k + 1 < BLOCKS:
+                nc.sync.dma_start(window[k + 1][:], table_blocks[:, k + 1, :])
             nc.sync.dma_start(column_w[k][:], wc_blocks[:, k, :])
+            if k + 1 < BLOCKS:
+                nc.sync.dma_start(dense_w[k + 1][:], wd_blocks[:, k + 1, :])
 
         total = [sums.tile([P, N], F32, name=f"total{b}") for b in range(BLOCKS)]
 
@@ -51,15 +53,8 @@ def tile_fusionlayer_kernel(tc, hidden, table, wd, bd, wc, bc, offs, out):
 
         for k in range(BLOCKS):
             for b in range(BLOCKS):
-                nc.tensor.matmul(
-                    total[b][:],
-                    dense_w[k // HALF][:, k % HALF, b * P : (b + 1) * P],
-                    tokens[:, k, :],
-                    start=False,
-                    stop=False,
-                )
+                nc.tensor.matmul(total[b][:], dense_w[k][:, b * P : (b + 1) * P], tokens[:, k, :], start=False, stop=False)
 
-        for k in range(BLOCKS):
             picked = held.tile([P, N], F32, name=f"picked{k}")
             nc.scalar.activation(picked[:], window[k][:].indirect(offsets[:]), COPY)
             picked_bf = held.tile([P, N], BF16, name=f"picked_bf{k}")

@@ -27,6 +27,9 @@ def tile_fusionlayer_kernel(tc, hidden, table, wd, bd, wc, bc, offs, out):
         ones = held.tile([2, N], F32, name="ones")
         nc.vector.memset(ones[:], 1.0)
 
+        warmed = held.tile([2, 1], F32, name="warmed")
+        nc.scalar.activation(warmed[:], ones[:, 0:1], GELU)
+
         tokens = held.tile([P, BLOCKS, N], BF16, name="tokens")
         nc.sync.dma_start(tokens[:], hidden.rearrange("(p k) j -> p k j", k=BLOCKS))
 
@@ -51,18 +54,17 @@ def tile_fusionlayer_kernel(tc, hidden, table, wd, bd, wc, bc, offs, out):
         for b in range(BLOCKS):
             nc.tensor.matmul(total[b][:], bias_rows[:, b * P : (b + 1) * P], ones[:], start=True, stop=False)
 
-        for k in range(BLOCKS):
+        def add_products(weights, moving, last):
             for b in range(BLOCKS):
-                nc.tensor.matmul(total[b][:], dense_w[k][:, b * P : (b + 1) * P], tokens[:, k, :], start=False, stop=False)
+                nc.tensor.matmul(total[b][:], weights[:, b * P : (b + 1) * P], moving, start=False, stop=last)
 
+        for k in range(BLOCKS):
+            add_products(dense_w[k], tokens[:, k, :], last=False)
             picked = held.tile([P, N], F32, name=f"picked{k}")
             nc.scalar.activation(picked[:], window[k][:].indirect(offsets[:]), COPY)
             picked_bf = held.tile([P, N], BF16, name=f"picked_bf{k}")
             nc.vector.tensor_copy(picked_bf[:], picked[:])
-            for b in range(BLOCKS):
-                nc.tensor.matmul(
-                    total[b][:], column_w[k][:, b * P : (b + 1) * P], picked_bf[:], start=False, stop=(k == BLOCKS - 1)
-                )
+            add_products(column_w[k], picked_bf[:], last=(k == BLOCKS - 1))
 
         for b in range(BLOCKS):
             result = held.tile([P, N], F32, name=f"result{b}")

@@ -40,11 +40,11 @@ def tile_fusionlayer_kernel(tc, hidden, table, wd, bd, wc, bc, offs, out):
         dense_w = [held.tile([P, C], BF16, name=f"dense_w{k}") for k in range(BLOCKS)]
         column_w = [held.tile([P, C], BF16, name=f"column_w{k}") for k in range(BLOCKS)]
 
-        nc.sync.dma_start(window[0][:], table_blocks[:, 0, :])
+        nc.scalar.dma_start(window[0][:], table_blocks[:, 0, :])
         nc.sync.dma_start(dense_w[0][:], wd_blocks[:, 0, :])
         for k in range(BLOCKS):
             if k + 1 < BLOCKS:
-                nc.sync.dma_start(window[k + 1][:], table_blocks[:, k + 1, :])
+                nc.scalar.dma_start(window[k + 1][:], table_blocks[:, k + 1, :])
             nc.sync.dma_start(column_w[k][:], wc_blocks[:, k, :])
             if k + 1 < BLOCKS:
                 nc.sync.dma_start(dense_w[k + 1][:], wd_blocks[:, k + 1, :])

@@ -27,9 +27,6 @@ def tile_fusionlayer_kernel(tc, hidden, table, wd, bd, wc, bc, offs, out):
         ones = held.tile([2, N], F32, name="ones")
         nc.vector.memset(ones[:], 1.0)
 
-        warmed = held.tile([2, 1], F32, name="warmed")
-        nc.scalar.activation(warmed[:], ones[:, 0:1], GELU)
-
         tokens = held.tile([P, BLOCKS, N], BF16, name="tokens")
         nc.sync.dma_start(tokens[:], hidden.rearrange("(p k) j -> p k j", k=BLOCKS))
 

@@ -38,13 +38,11 @@ def tile_fusionlayer_kernel(tc, hidden, table, wd, bd, wc, bc, offs, out):
         column_w = [held.tile([P, C], BF16, name=f"column_w{k}") for k in range(BLOCKS)]
 
         nc.scalar.dma_start(window[0][:], table_blocks[:, 0, :])
+        nc.scalar.dma_start(window[1][:], table_blocks[:, 1, :])
         nc.sync.dma_start(dense_w[0][:], wd_blocks[:, 0, :])
-        for k in range(BLOCKS):
-            if k + 1 < BLOCKS:
-                nc.scalar.dma_start(window[k + 1][:], table_blocks[:, k + 1, :])
-            nc.sync.dma_start(column_w[k][:], wc_blocks[:, k, :])
-            if k + 1 < BLOCKS:
-                nc.sync.dma_start(dense_w[k + 1][:], wd_blocks[:, k + 1, :])
+
+        warmed = held.tile([2, 1], F32, name="warmed")
+        nc.scalar.activation(warmed[:], ones[:, 0:1], GELU)
 
         total = [sums.tile([P, N], F32, name=f"total{b}") for b in range(BLOCKS)]
 
@@ -56,6 +54,12 @@ def tile_fusionlayer_kernel(tc, hidden, table, wd, bd, wc, bc, offs, out):
                 nc.tensor.matmul(total[b][:], weights[:, b * P : (b + 1) * P], moving, start=False, stop=last)
 
         for k in range(BLOCKS):
+            if k + 2 < BLOCKS:
+                nc.scalar.dma_start(window[k + 2][:], table_blocks[:, k + 2, :])
+            nc.sync.dma_start(column_w[k][:], wc_blocks[:, k, :])
+            if k + 1 < BLOCKS:
+                nc.sync.dma_start(dense_w[k + 1][:], wd_blocks[:, k + 1, :])
+
             add_products(dense_w[k], tokens[:, k, :], last=False)
             picked = held.tile([P, N], F32, name=f"picked{k}")
             nc.scalar.activation(picked[:], window[k][:].indirect(offsets[:]), COPY)

@@ -24,7 +24,7 @@ def tile_fusionlayer_kernel(tc, hidden, table, wd, bd, wc, bc, offs, out):
         bias_rows = held.tile([2, C], F32, name="bias_rows")
         nc.sync.dma_start(bias_rows[0:1, :], bd.rearrange("m o -> o m"))
         nc.sync.dma_start(bias_rows[1:2, :], bc.rearrange("m o -> o m"))
-        ones = held.tile([2, N], F32, name="ones")
+        ones = held.tile([2, 1], F32, name="ones")
         nc.vector.memset(ones[:], 1.0)
 
         tokens = held.tile([P, BLOCKS, N], BF16, name="tokens")
@@ -42,25 +42,29 @@ def tile_fusionlayer_kernel(tc, hidden, table, wd, bd, wc, bc, offs, out):
         nc.sync.dma_start(dense_w[0][:], wd_blocks[:, 0, :])
 
         warmed = held.tile([2, 1], F32, name="warmed")
-        nc.scalar.activation(warmed[:], ones[:, 0:1], GELU)
+        nc.scalar.activation(warmed[:], ones[:], GELU)
+
+        bias_turned = sums.tile([P, BLOCKS], F32, name="bias_turned")
+        for b in range(BLOCKS):
+            nc.tensor.matmul(bias_turned[:, b : b + 1], bias_rows[:, b * P : (b + 1) * P], ones[:], start=True, stop=True)
+        bias = held.tile([P, BLOCKS], F32, name="bias")
+        nc.vector.tensor_copy(bias[:], bias_turned[:])
 
         total = [sums.tile([P, N], F32, name=f"total{b}") for b in range(BLOCKS)]
 
-        for b in range(BLOCKS):
-            nc.tensor.matmul(total[b][:], bias_rows[:, b * P : (b + 1) * P], ones[:], start=True, stop=False)
-
-        def add_products(weights, moving, last):
+        def add_products(weights, moving, first=False, last=False):
             for b in range(BLOCKS):
-                nc.tensor.matmul(total[b][:], weights[:, b * P : (b + 1) * P], moving, start=False, stop=last)
+                nc.tensor.matmul(total[b][:], weights[:, b * P : (b + 1) * P], moving, start=first, stop=last)
 
         for k in range(BLOCKS):
             if k + 2 < BLOCKS:
-                nc.scalar.dma_start(window[k + 2][:], table_blocks[:, k + 2, :])
+                table_queue = nc.scalar if k + 2 < BLOCKS - 1 else nc.sync
+                table_queue.dma_start(window[k + 2][:], table_blocks[:, k + 2, :])
             nc.sync.dma_start(column_w[k][:], wc_blocks[:, k, :])
             if k + 1 < BLOCKS:
                 nc.sync.dma_start(dense_w[k + 1][:], wd_blocks[:, k + 1, :])
 
-            add_products(dense_w[k], tokens[:, k, :], last=False)
+            add_products(dense_w[k], tokens[:, k, :], first=(k == 0))
             picked = held.tile([P, N], F32, name=f"picked{k}")
             nc.scalar.activation(picked[:], window[k][:].indirect(offsets[:]), COPY)
             picked_bf = held.tile([P, N], BF16, name=f"picked_bf{k}")
@@ -69,5 +73,5 @@ def tile_fusionlayer_kernel(tc, hidden, table, wd, bd, wc, bc, offs, out):
 
         for b in range(BLOCKS):
             result = held.tile([P, N], F32, name=f"result{b}")
-            nc.scalar.activation(result[:], total[b][:], GELU)
+            nc.scalar.activation(result[:], total[b][:], GELU, bias=bias[:, b : b + 1])
             nc.sync.dma_start(out[b * P : (b + 1) * P, :], result[:])

@@ -8,6 +8,7 @@ C = 768
 S = 1024
 N = 128
 BLOCKS = C // P
+HALF = BLOCKS // 2
 
 FLOPS = 2 * 2 * C * C * N
 
@@ -18,6 +19,17 @@ def tile_fusionlayer_kernel(tc, hidden, table, wd, bd, wc, bc, offs, out):
         tc.tile_pool(name="held", bufs=1) as held,
         tc.psum_pool(name="sums", bufs=1) as sums,
     ):
+        table_blocks = table.rearrange("(p k) s -> p k s", k=BLOCKS)
+        wd_blocks = wd.rearrange("(p k) m -> p k m", k=BLOCKS)
+        wc_blocks = wc.rearrange("(p k) m -> p k m", k=BLOCKS)
+
+        window = [held.tile([P, S], F32, name=f"window{k}") for k in range(BLOCKS)]
+
+        def load_weights(name, blocks, first, count):
+            weights = held.tile([P, count, C], BF16, name=f"{name}{first}")
+            nc.sync.dma_start(weights[:], blocks[:, first : first + count, :])
+            return [weights[:, i, :] for i in range(count)]
+
         offsets = held.tile([P, N // 16], U16, name="offsets")
         nc.sync.dma_start(offsets[:], offs)
 
@@ -29,17 +41,10 @@ def tile_fusionlayer_kernel(tc, hidden, table, wd, bd, wc, bc, offs, out):
 
         tokens = held.tile([P, BLOCKS, N], BF16, name="tokens")
         nc.sync.dma_start(tokens[:], hidden.rearrange("(p k) j -> p k j", k=BLOCKS))
-
-        table_blocks = table.rearrange("(p k) s -> p k s", k=BLOCKS)
-        wd_blocks = wd.rearrange("(p k) m -> p k m", k=BLOCKS)
-        wc_blocks = wc.rearrange("(p k) m -> p k m", k=BLOCKS)
-        window = [held.tile([P, S], F32, name=f"window{k}") for k in range(BLOCKS)]
-        dense_w = [held.tile([P, C], BF16, name=f"dense_w{k}") for k in range(BLOCKS)]
-        column_w = [held.tile([P, C], BF16, name=f"column_w{k}") for k in range(BLOCKS)]
-
         nc.scalar.dma_start(window[0][:], table_blocks[:, 0, :])
         nc.scalar.dma_start(window[1][:], table_blocks[:, 1, :])
-        nc.sync.dma_start(dense_w[0][:], wd_blocks[:, 0, :])
+
+        dense_w = load_weights("dense_w", wd_blocks, 0, HALF)
 
         warmed = held.tile([2, 1], F32, name="warmed")
         nc.scalar.activation(warmed[:], ones[:], GELU)
@@ -56,20 +61,28 @@ def tile_fusionlayer_kernel(tc, hidden, table, wd, bd, wc, bc, offs, out):
             for b in range(BLOCKS):
                 nc.tensor.matmul(total[b][:], weights[:, b * P : (b + 1) * P], moving, start=first, stop=last)
 
-        for k in range(BLOCKS):
-            if k + 2 < BLOCKS:
-                table_queue = nc.scalar if k + 2 < BLOCKS - 1 else nc.sync
-                table_queue.dma_start(window[k + 2][:], table_blocks[:, k + 2, :])
-            nc.sync.dma_start(column_w[k][:], wc_blocks[:, k, :])
-            if k + 1 < BLOCKS:
-                nc.sync.dma_start(dense_w[k + 1][:], wd_blocks[:, k + 1, :])
-
-            add_products(dense_w[k], tokens[:, k, :], first=(k == 0))
+        def look_up(k):
             picked = held.tile([P, N], F32, name=f"picked{k}")
             nc.scalar.activation(picked[:], window[k][:].indirect(offsets[:]), COPY)
             picked_bf = held.tile([P, N], BF16, name=f"picked_bf{k}")
             nc.vector.tensor_copy(picked_bf[:], picked[:])
-            add_products(column_w[k], picked_bf[:], last=(k == BLOCKS - 1))
+            return picked_bf
+
+        for k in range(HALF):
+            add_products(dense_w[k], tokens[:, k, :], first=(k == 0))
+        column_w = load_weights("column_w", wc_blocks, 0, HALF)
+        dense_w += load_weights("dense_w", wd_blocks, HALF, HALF)
+        for k in range(HALF):
+            nc.scalar.dma_start(window[k + 2][:], table_blocks[:, k + 2, :])
+            add_products(column_w[k], look_up(k)[:])
+
+        nc.sync.dma_start(window[BLOCKS - 1][:], table_blocks[:, BLOCKS - 1, :])
+        for k in range(HALF, BLOCKS):
+            column_w += load_weights("column_w", wc_blocks, k, 1)
+        for k in range(HALF, BLOCKS):
+            add_products(dense_w[k], tokens[:, k, :])
+        for k in range(HALF, BLOCKS):
+            add_products(column_w[k], look_up(k)[:], last=(k == BLOCKS - 1))
 
         for b in range(BLOCKS):
             result = held.tile([P, N], F32, name=f"result{b}")

@@ -72,11 +72,11 @@ def tile_fusionlayer_kernel(tc, hidden, table, wd, bd, wc, bc, offs, out):
             add_products(dense_w[k], tokens[:, k, :], first=(k == 0))
         column_w = load_weights("column_w", wc_blocks, 0, HALF)
         dense_w += load_weights("dense_w", wd_blocks, HALF, HALF)
-        for k in range(HALF):
-            nc.scalar.dma_start(window[k + 2][:], table_blocks[:, k + 2, :])
+        for k, ahead in zip(range(HALF), (2, 3, 5)):
+            nc.scalar.dma_start(window[ahead][:], table_blocks[:, ahead, :])
             add_products(column_w[k], look_up(k)[:])
 
-        nc.sync.dma_start(window[BLOCKS - 1][:], table_blocks[:, BLOCKS - 1, :])
+        nc.sync.dma_start(window[4][:], table_blocks[:, 4, :])
         for k in range(HALF, BLOCKS):
             column_w += load_weights("column_w", wc_blocks, k, 1)
         for k in range(HALF, BLOCKS):

@@ -77,14 +77,23 @@ def tile_fusionlayer_kernel(tc, hidden, table, wd, bd, wc, bc, offs, out):
             add_products(column_w[k], look_up(k)[:])
 
         nc.sync.dma_start(window[4][:], table_blocks[:, 4, :])
-        for k in range(HALF, BLOCKS):
-            column_w += load_weights("column_w", wc_blocks, k, 1)
+
+        column_w_late = []
+        for side in range(2):
+            late = held.tile([P, HALF, HALF * P], BF16, name=f"column_w_late{side}")
+            nc.sync.dma_start(late[:], wc_blocks[:, HALF:BLOCKS, side * HALF * P : (side + 1) * HALF * P])
+            column_w_late.append(late)
+
         for k in range(HALF, BLOCKS):
             add_products(dense_w[k], tokens[:, k, :])
-        for k in range(HALF, BLOCKS):
-            add_products(column_w[k], look_up(k)[:], last=(k == BLOCKS - 1))
+        picked_late = [look_up(k) for k in range(HALF, BLOCKS)]
 
         for b in range(BLOCKS):
+            side, i = divmod(b, HALF)
+            for k in range(HALF):
+                nc.tensor.matmul(
+                    total[b][:], column_w_late[side][:, k, i * P : (i + 1) * P], picked_late[k][:], start=False, stop=(k == HALF - 1)
+                )
             result = held.tile([P, N], F32, name=f"result{b}")
             nc.scalar.activation(result[:], total[b][:], GELU, bias=bias[:, b : b + 1])
             nc.sync.dma_start(out[b * P : (b + 1) * P, :], result[:])

@@ -72,11 +72,11 @@ def tile_fusionlayer_kernel(tc, hidden, table, wd, bd, wc, bc, offs, out):
             add_products(dense_w[k], tokens[:, k, :], first=(k == 0))
         column_w = load_weights("column_w", wc_blocks, 0, HALF)
         dense_w += load_weights("dense_w", wd_blocks, HALF, HALF)
-        for k, ahead in zip(range(HALF), (2, 3, 5)):
-            nc.scalar.dma_start(window[ahead][:], table_blocks[:, ahead, :])
+        for k in range(HALF):
+            nc.scalar.dma_start(window[k + 2][:], table_blocks[:, k + 2, :])
             add_products(column_w[k], look_up(k)[:])
 
-        nc.sync.dma_start(window[4][:], table_blocks[:, 4, :])
+        nc.sync.dma_start(window[BLOCKS - 1][:], table_blocks[:, BLOCKS - 1, :])
 
         column_w_late = []
         for side in range(2):

import concourse.mybir as mybir

BF16, F32, U16 = mybir.dt.bfloat16, mybir.dt.float32, mybir.dt.uint16
COPY, GELU = mybir.ActivationFunctionType.Copy, mybir.ActivationFunctionType.Gelu

P = 128
C = 768
S = 1024
N = 128
BLOCKS = C // P
HALF = BLOCKS // 2

FLOPS = 2 * 2 * C * C * N


def tile_fusionlayer_kernel(tc, hidden, table, wd, bd, wc, bc, offs, out):
    nc = tc.nc
    with (
        tc.tile_pool(name="held", bufs=1) as held,
        tc.psum_pool(name="sums", bufs=1) as sums,
    ):
        table_blocks = table.rearrange("(p k) s -> p k s", k=BLOCKS)
        wd_blocks = wd.rearrange("(p k) m -> p k m", k=BLOCKS)
        wc_blocks = wc.rearrange("(p k) m -> p k m", k=BLOCKS)

        window = [held.tile([P, S], F32, name=f"window{k}") for k in range(BLOCKS)]

        def load_weights(name, blocks, first, count):
            weights = held.tile([P, count, C], BF16, name=f"{name}{first}")
            nc.sync.dma_start(weights[:], blocks[:, first : first + count, :])
            return [weights[:, i, :] for i in range(count)]

        offsets = held.tile([P, N // 16], U16, name="offsets")
        nc.sync.dma_start(offsets[:], offs)

        bias_rows = held.tile([2, C], F32, name="bias_rows")
        nc.sync.dma_start(bias_rows[0:1, :], bd.rearrange("m o -> o m"))
        nc.sync.dma_start(bias_rows[1:2, :], bc.rearrange("m o -> o m"))
        ones = held.tile([2, 1], F32, name="ones")
        nc.vector.memset(ones[:], 1.0)

        tokens = held.tile([P, BLOCKS, N], BF16, name="tokens")
        nc.sync.dma_start(tokens[:], hidden.rearrange("(p k) j -> p k j", k=BLOCKS))
        nc.scalar.dma_start(window[0][:], table_blocks[:, 0, :])
        nc.scalar.dma_start(window[1][:], table_blocks[:, 1, :])

        dense_w = load_weights("dense_w", wd_blocks, 0, HALF)

        warmed = held.tile([2, 1], F32, name="warmed")
        nc.scalar.activation(warmed[:], ones[:], GELU)

        bias_turned = sums.tile([P, BLOCKS], F32, name="bias_turned")
        for b in range(BLOCKS):
            nc.tensor.matmul(bias_turned[:, b : b + 1], bias_rows[:, b * P : (b + 1) * P], ones[:], start=True, stop=True)
        bias = held.tile([P, BLOCKS], F32, name="bias")
        nc.vector.tensor_copy(bias[:], bias_turned[:])

        total = [sums.tile([P, N], F32, name=f"total{b}") for b in range(BLOCKS)]

        def add_products(weights, moving, first=False, last=False):
            for b in range(BLOCKS):
                nc.tensor.matmul(total[b][:], weights[:, b * P : (b + 1) * P], moving, start=first, stop=last)

        def look_up(k):
            picked = held.tile([P, N], F32, name=f"picked{k}")
            nc.scalar.activation(picked[:], window[k][:].indirect(offsets[:]), COPY)
            picked_bf = held.tile([P, N], BF16, name=f"picked_bf{k}")
            nc.vector.tensor_copy(picked_bf[:], picked[:])
            return picked_bf

        for k in range(HALF):
            add_products(dense_w[k], tokens[:, k, :], first=(k == 0))
        column_w = load_weights("column_w", wc_blocks, 0, HALF)
        dense_w += load_weights("dense_w", wd_blocks, HALF, HALF)
        for k in range(HALF):
            nc.scalar.dma_start(window[k + 2][:], table_blocks[:, k + 2, :])
            add_products(column_w[k], look_up(k)[:])

        nc.sync.dma_start(window[BLOCKS - 1][:], table_blocks[:, BLOCKS - 1, :])

        column_w_late = []
        for side in range(2):
            late = held.tile([P, HALF, HALF * P], BF16, name=f"column_w_late{side}")
            nc.sync.dma_start(late[:], wc_blocks[:, HALF:BLOCKS, side * HALF * P : (side + 1) * HALF * P])
            column_w_late.append(late)

        for k in range(HALF, BLOCKS):
            add_products(dense_w[k], tokens[:, k, :])
        picked_late = [look_up(k) for k in range(HALF, BLOCKS)]

        for b in range(BLOCKS):
            side, i = divmod(b, HALF)
            for k in range(HALF):
                nc.tensor.matmul(
                    total[b][:], column_w_late[side][:, k, i * P : (i + 1) * P], picked_late[k][:], start=False, stop=(k == HALF - 1)
                )
            result = held.tile([P, N], F32, name=f"result{b}")
            nc.scalar.activation(result[:], total[b][:], GELU, bias=bias[:, b : b + 1])
            nc.sync.dma_start(out[b * P : (b + 1) * P, :], result[:])
